import numpy as np
import ml_dtypes


def mxq(x, axis, fmt="e4m3"):
    dtype, down = {"e4m3": (ml_dtypes.float8_e4m3fn, 7), "e5m2": (ml_dtypes.float8_e5m2, 14)}[fmt]
    v = np.moveaxis(np.asarray(x, np.float32).astype(ml_dtypes.bfloat16).astype(np.float64), axis, -1)
    blocks = v.reshape(v.shape[:-1] + (-1, 32))
    amax = np.abs(blocks).max(-1, keepdims=True)
    byte = np.maximum(np.where(amax > 0, np.frexp(amax)[1] - 1 + 127, 0) - down, 1)
    scale = np.exp2(byte - 127.0)
    codes = (blocks / scale).astype(np.float32).astype(dtype).astype(np.float64)
    return np.moveaxis((codes * scale).reshape(v.shape), -1, axis)


WIDE = False


def mx_kscale(k):
    if not WIDE:
        return np.ones(k)
    levels = np.array([10, -10, 5, -5, 0])
    if k % 512:
        return np.exp2(np.random.permutation(np.resize(levels, k // 32))).repeat(32)
    a = np.empty((k // 512, 16))
    for p in range(k // 512):
        a[p, :8] = np.random.permutation(np.resize(levels, 8))
        for g in range(8):
            far = levels[np.abs(levels - a[p, g]) >= 10]
            a[p, g + 8] = far[np.random.randint(len(far))]
    return np.exp2(a.ravel()).repeat(32)


BF16 = ml_dtypes.bfloat16


def bf(x):
    return np.asarray(x, np.float32).astype(BF16)


def f64(x):
    return np.asarray(x).astype(np.float64)


B, F, M, N, H, O = 1, 128, 128, 128, 512, 128
BN_EPS = 1e-5


def bn(x, g, b, m, v):
    sh = [1] * x.ndim
    sh[1] = -1
    return g.reshape(sh) * (x - m.reshape(sh)) * (1.0 / np.sqrt(v.reshape(sh) + BN_EPS)) + b.reshape(sh)


def setup_inputs():
    s = mx_kscale(H)
    k = mx_kscale(H)
    return {"h2": bf(np.maximum(np.random.standard_normal((B, H, M, N)), 0.0) * s[None, :, None, None]),
            "W3": bf(np.random.standard_normal((H, H)) * 1.4 / np.sqrt(H) / s[None, :]),
            "g3": bf((1.0 + 0.1 * np.random.standard_normal(H)) * k),
            "b3": bf(0.2 * np.random.standard_normal(H) * k),
            "m3": bf(0.2 * np.random.standard_normal(H)),
            "v3": bf(np.random.uniform(0.5, 1.5, H)),
            "Wc1": bf(np.random.standard_normal((H, H)) * 0.4 / np.sqrt(H) / k[None, :]),
            "gc1": bf(1.0 + 0.1 * np.random.standard_normal(H)),
            "bc1": bf(0.2 * np.random.standard_normal(H)),
            "mc1": bf(0.2 * np.random.standard_normal(H)),
            "vc1": bf(np.random.uniform(0.5, 1.5, H))}


def reference(h2, W3, g3, b3, m3, v3, Wc1, gc1, bc1, mc1, vc1):
    x3 = (mxq(f64(W3), 1, "e4m3") @ mxq(f64(h2).reshape(B, H, M * N), 1, "e4m3")).reshape(B, H, M, N)
    h3 = np.maximum(bn(x3, f64(g3), f64(b3), f64(m3), f64(v3)), 0.0)
    p = h3.max(axis=2)
    xc = mxq(f64(Wc1), 1, "e4m3") @ mxq(p, 1, "e4m3")
    return np.maximum(bn(xc, f64(gc1), f64(bc1), f64(mc1), f64(vc1)), 0.0)

@@ -1,0 +1,328 @@
+from contextlib import ExitStack
+
+import concourse.mybir as mybir
+from concourse.masks import make_identity
+
+F32 = mybir.dt.float32
+BF16 = mybir.dt.bfloat16
+U32 = mybir.dt.uint32
+U8 = mybir.dt.uint8
+FP8X4 = mybir.dt.float8_e4m3fn_x4
+ALU = mybir.AluOpType
+ACT = mybir.ActivationFunctionType
+
+P = 128
+PACK = 4
+H = 512
+NPTS = 128
+COLS = NPTS * NPTS
+UNIT = 512
+UNITS = COLS // UNIT
+SHORT_LOADS = 6
+LOADS = (UNIT,) * SHORT_LOADS + (2 * UNIT,) * ((UNITS - SHORT_LOADS) // 2)
+WC1_LOAD_AT = 12 * UNIT
+BANKS = UNITS * PACK
+AHEAD = 6
+GROUPED_BUFS = 2
+S_COLS = 336
+BN_EPS = 1e-5
+WC1_AT = 48
+EARLY = 3
+
+FLOPS = 2 * H * H * (COLS + NPTS)
+
+
+def tile_p2b_xcorr_pb_kernel(tc, h2, W3, g3, b3, m3, v3, Wc1, gc1, bc1, mc1, vc1, out):
+    nc = tc.nc
+    with ExitStack() as ctx:
+        keep = ctx.enter_context(tc.tile_pool(name="keep", bufs=1))
+        rawp = ctx.enter_context(tc.tile_pool(name="rawp", bufs=1))
+        grpp = ctx.enter_context(tc.tile_pool(name="grpp", bufs=GROUPED_BUFS))
+        codp = ctx.enter_context(tc.tile_pool(name="codp", bufs=3))
+        psum = ctx.enter_context(tc.psum_pool(name="psum", bufs=AHEAD))
+        ctx.enter_context(tc.manual_schedule())
+
+        prm = keep.tile([P, 8, 16], BF16)
+
+        def load_vector(queue, slot, vec):
+            queue.dma_start(out=prm[:, slot, 0:PACK], in_=vec.rearrange("(p t) -> p t", t=PACK))
+
+        load_vector(nc.scalar, 0, g3)
+        load_vector(nc.scalar, 6, v3)
+        load_vector(nc.scalar, 2, b3)
+        load_vector(nc.scalar, 4, m3)
+
+        ident = keep.tile([P, P], F32)
+        make_identity(nc, ident[:])
+        load_vector(nc.gpsimd, 7, vc1)
+        load_vector(nc.gpsimd, 1, gc1)
+        load_vector(nc.gpsimd, 3, bc1)
+        load_vector(nc.gpsimd, 5, mc1)
+
+        w3_rows = keep.tile([P, PACK, H], BF16)
+        nc.sync.dma_start(out=w3_rows[:], in_=W3.rearrange("(m t) h -> m t h", t=PACK))
+        wc1_rows = keep.tile([P, PACK, H], BF16)
+
+        h2_rows = h2[0].rearrange("(p j) m n -> p j (m n)", j=PACK)
+        raw_of = {}
+        first = 0
+        for width in LOADS:
+            raw = rawp.tile([P, PACK, width], BF16, tag="raw%d" % width, bufs=SHORT_LOADS if width == UNIT else len(LOADS) - SHORT_LOADS)
+            nc.sync.dma_start(out=raw[:], in_=h2_rows[:, :, first : first + width])
+            for a in range(0, width, UNIT):
+                raw_of[(first + a) // UNIT] = (raw, a)
+            first += width
+            if first == WC1_LOAD_AT:
+                nc.sync.dma_start(out=wc1_rows[:], in_=Wc1.rearrange("(m t) h -> m t h", t=PACK))
+
+        one = keep.tile([P, 1], F32)
+        nc.vector.memset(one[:], 1.0)
+        warm = keep.tile([P, 1], F32)
+        nc.scalar.activation(out=warm[:], in_=one[:], func=ACT.Sqrt)
+
+        sign = keep.tile([P, PACK], F32)
+        nc.vector.tensor_scalar(out=sign[:], in0=prm[:, 0, 0:PACK], scalar1=0.0, scalar2=2.0, op0=ALU.is_ge, op1=ALU.mult)
+        nc.vector.tensor_scalar(out=sign[:], in0=sign[:], scalar1=-1.0, scalar2=None, op0=ALU.add)
+
+        var_eps, std, rough, newton, rstd, gain, shift = {}, {}, {}, {}, {}, {}, {}
+        for k in range(2):
+            var_eps[k] = keep.tile([P, PACK], F32, name="var_eps%d" % k)
+            std[k] = keep.tile([P, PACK], F32, name="std%d" % k)
+            rough[k] = keep.tile([P, PACK], F32, name="rough%d" % k)
+            newton[k] = keep.tile([P, PACK], F32, name="newton%d" % k)
+            rstd[k] = keep.tile([P, PACK], F32, name="rstd%d" % k)
+            gain[k] = keep.tile([P, PACK], F32, name="gain%d" % k)
+            shift[k] = keep.tile([P, PACK], F32, name="shift%d" % k)
+        gain_abs = keep.tile([P, PACK], F32)
+
+        def norm_root(k):
+            nc.gpsimd.tensor_scalar(
+                out=var_eps[k][:], in0=prm[:, 6 + k, 0:PACK], scalar1=1.0, scalar2=BN_EPS, op0=ALU.mult, op1=ALU.add
+            )
+            nc.scalar.activation(out=std[k][:], in_=var_eps[k][:], func=ACT.Sqrt)
+
+        def norm_reciprocal(k):
+            nc.vector.reciprocal(out=rough[k][:], in_=std[k][:])
+
+        def norm_gain_shift(k):
+            tt = nc.gpsimd.tensor_tensor
+            tt(out=newton[k][:], in0=rough[k][:], in1=rough[k][:], op=ALU.mult)
+            tt(out=newton[k][:], in0=newton[k][:], in1=var_eps[k][:], op=ALU.mult)
+            nc.gpsimd.tensor_scalar(out=newton[k][:], in0=newton[k][:], scalar1=-0.5, scalar2=1.5, op0=ALU.mult, op1=ALU.add)
+            tt(out=rstd[k][:], in0=rough[k][:], in1=newton[k][:], op=ALU.mult)
+            tt(out=gain[k][:], in0=prm[:, k, 0:PACK], in1=rstd[k][:], op=ALU.mult)
+            tt(out=shift[k][:], in0=prm[:, 4 + k, 0:PACK], in1=gain[k][:], op=ALU.mult)
+            tt(out=shift[k][:], in0=prm[:, 2 + k, 0:PACK], in1=shift[k][:], op=ALU.subtract)
+
+        norm_root(0)
+        norm_reciprocal(0)
+        norm_gain_shift(0)
+        nc.gpsimd.tensor_tensor(out=gain_abs[:], in0=gain[0][:], in1=sign[:], op=ALU.mult)
+
+        w3_signed = keep.tile([P, PACK, H], BF16)
+        for t in range(PACK):
+            nc.vector.tensor_scalar(
+                out=w3_signed[:, t, :], in0=w3_rows[:, t, :], scalar1=sign[:, t : t + 1], scalar2=None, op0=ALU.mult
+            )
+
+        def turn_weights(rows):
+            halves = []
+            for b in range(2):
+                turned = psum.tile([P, 2, 2, P], F32, tag="aux", bufs=2)
+                for i in range(2):
+                    words = rows[:, 2 * b + i, :].bitcast(F32)
+                    for u in range(2):
+                        nc.tensor.transpose(turned[:, i, u, :], words[:, u : H // 2 : 2], ident[:])
+                halves.append(turned)
+            return halves
+
+        def group_weights(halves, copy):
+            grouped_w = keep.tile([P, PACK * H], BF16, align_bytes=64)
+            words_out = grouped_w[:].bitcast(F32).rearrange("p (t m u) -> p t m u", t=PACK, u=2)
+            for b in range(2):
+                copy(out=words_out[:, 2 * b : 2 * b + 2, :, :], in_=halves[b][:].rearrange("p t u m -> p t m u"))
+            return grouped_w
+
+        def quantize_weights(grouped_w, codes, scales):
+            nc.vector.quantize_mx(out=codes[:].bitcast(FP8X4), scales=scales[:], in_=grouped_w[:])
+
+        w3_codes = keep.tile([P, H], U32, align_bytes=64)
+        w3_scales = keep.tile([P, H], U8, align_bytes=64)
+        wc1_codes = keep.tile([P, H], U32, align_bytes=64)
+        wc1_scales = keep.tile([P, H], U8, align_bytes=64)
+        w3_grouped = group_weights(turn_weights(w3_signed), nc.vector.tensor_copy)
+
+        grouped_of = {}
+        codes_of = {}
+        bank_of = {}
+
+        def rows_of(u):
+            raw, a = raw_of[u]
+            return raw[:, :, a : a + UNIT].rearrange("p j c -> p c j")
+
+        def interleave_most(u):
+            grouped = grpp.tile([P, UNIT, PACK], BF16, tag="grouped", align_bytes=64)
+            nc.scalar.copy(out=grouped[:, 0:S_COLS, :], in_=rows_of(u)[:, 0:S_COLS, :])
+            grouped_of[u] = grouped
+
+        def interleave_rest(u):
+            if u < GROUPED_BUFS:
+                nc.vector.tensor_copy(out=grouped_of[u][:, S_COLS:UNIT, :], in_=rows_of(u)[:, S_COLS:UNIT, :])
+            else:
+                nc.gpsimd.tensor_scalar(
+                    out=grouped_of[u][:, S_COLS:UNIT, :],
+                    in0=rows_of(u)[:, S_COLS:UNIT, :],
+                    scalar1=1.0,
+                    scalar2=0.0,
+                    op0=ALU.mult,
+                    op1=ALU.add,
+                )
+
+        def interleave(u):
+            interleave_most(u)
+            interleave_rest(u)
+
+        def quantize(u):
+            codes = codp.tile([P, UNIT], U32, tag="codes", align_bytes=64)
+            scales = codp.tile([P, UNIT], U8, tag="scales", align_bytes=64)
+            nc.vector.quantize_mx(
+                out=codes[:].bitcast(FP8X4), scales=scales[:], in_=grouped_of[u][:].rearrange("p c j -> p (c j)")
+            )
+            codes_of[u] = (codes, scales)
+
+        def multiply(s):
+            u, t = divmod(s, PACK)
+            codes, scales = codes_of[u]
+            bank = psum.tile([P, UNIT], F32, tag="x3")
+            nc.tensor.matmul_mx(
+                out=bank[:],
+                lhsT=w3_codes[:, t * P : (t + 1) * P].bitcast(FP8X4),
+                lhsT_scale=w3_scales[:, t * P : (t + 1) * P],
+                rhs=codes[:].bitcast(FP8X4),
+                rhs_scale=scales[:],
+                start=True,
+                stop=True,
+            )
+            bank_of[s] = bank
+
+        top = keep.tile([P, PACK, UNIT], F32)
+        top_h3 = keep.tile([P, PACK, UNIT], BF16)
+        started = set()
+        fresh = []
+        ripe = []
+
+        def running_max(what, acc, t, new):
+            if (what, t) in started:
+                nc.vector.tensor_tensor(out=acc[:, t, :], in0=new[:], in1=acc[:, t, :], op=ALU.max)
+            else:
+                nc.vector.tensor_copy(out=acc[:, t, :], in_=new[:])
+                started.add((what, t))
+
+        def scalar_reads(s):
+            return s % 3 == 2
+
+        def read_early(s):
+            if s < BANKS and scalar_reads(s):
+                t = s % PACK
+                h3 = keep.tile([P, UNIT], BF16, tag="h3", bufs=6)
+                nc.scalar.activation(
+                    out=h3[:], in_=bank_of[s][:], func=ACT.Relu, bias=shift[0][:, t : t + 1], scale=gain_abs[:, t : t + 1]
+                )
+                fresh.append((t, h3))
+
+        def fold():
+            for t, h3 in ripe:
+                running_max("h3", top_h3, t, h3)
+            ripe.clear()
+            ripe.extend(fresh)
+            fresh.clear()
+
+        def read_bank(s):
+            if not scalar_reads(s):
+                running_max("x3", top, s % PACK, bank_of[s])
+
+        for u in range(GROUPED_BUFS):
+            interleave_most(u)
+        interleave_rest(0)
+        quantize_weights(w3_grouped, w3_codes, w3_scales)
+        quantize(0)
+        interleave(GROUPED_BUFS)
+        for s in range(PACK):
+            multiply(s)
+        interleave_rest(1)
+        quantize(1)
+        interleave(GROUPED_BUFS + 1)
+        for s in range(PACK, AHEAD):
+            multiply(s)
+
+        for s in range(EARLY):
+            read_early(s)
+        for s in range(BANKS):
+            nxt = s + AHEAD
+            read_early(s + EARLY)
+            if nxt < BANKS and nxt % PACK == 0:
+                fold()
+                quantize(nxt // PACK)
+                if nxt // PACK + GROUPED_BUFS < UNITS:
+                    interleave(nxt // PACK + GROUPED_BUFS)
+            read_bank(s)
+            if nxt < BANKS:
+                multiply(nxt)
+            if s == WC1_AT:
+                wc1_halves = turn_weights(wc1_rows)
+                norm_root(1)
+            if s == WC1_AT + 2 * PACK:
+                wc1_grouped = group_weights(wc1_halves, nc.scalar.copy)
+                norm_reciprocal(1)
+            if s == WC1_AT + 5 * PACK:
+                quantize_weights(wc1_grouped, wc1_codes, wc1_scales)
+        norm_gain_shift(1)
+
+        fold()
+        fold()
+        half_h3 = keep.tile([P, PACK, 2 * NPTS], BF16)
+        nc.vector.tensor_tensor(out=half_h3[:], in0=top_h3[:, :, 0 : 2 * NPTS], in1=top_h3[:, :, 2 * NPTS : UNIT], op=ALU.max)
+        half = keep.tile([P, PACK, 2 * NPTS], F32)
+        peak = keep.tile([P, PACK, NPTS], F32)
+        pooled_x3 = keep.tile([P, PACK, NPTS], BF16)
+        for t in (0, 2):
+            nc.vector.tensor_tensor(
+                out=half[:, t : t + 2, :], in0=top[:, t : t + 2, 0 : 2 * NPTS], in1=top[:, t : t + 2, 2 * NPTS : UNIT], op=ALU.max
+            )
+        for t in (0, 2):
+            nc.vector.tensor_tensor(
+                out=peak[:, t : t + 2, :], in0=half[:, t : t + 2, 0:NPTS], in1=half[:, t : t + 2, NPTS : 2 * NPTS], op=ALU.max
+            )
+        for t in range(PACK):
+            nc.scalar.activation(
+                out=pooled_x3[:, t, :], in_=peak[:, t, :], func=ACT.Relu, bias=shift[0][:, t : t + 1], scale=gain_abs[:, t : t + 1]
+            )
+        peak_h3 = keep.tile([P, PACK, NPTS], BF16)
+        nc.vector.tensor_tensor(out=peak_h3[:], in0=half_h3[:, :, 0:NPTS], in1=half_h3[:, :, NPTS : 2 * NPTS], op=ALU.max)
+        pooled = keep.tile([P, PACK, NPTS], BF16)
+        nc.vector.tensor_tensor(out=pooled[:], in0=pooled_x3[:], in1=peak_h3[:], op=ALU.max)
+
+        p_grouped = keep.tile([P, NPTS, PACK], BF16, align_bytes=64)
+        nc.vector.tensor_copy(out=p_grouped[:], in_=pooled[:].rearrange("p t n -> p n t"))
+        p_codes = keep.tile([P, NPTS], U32, align_bytes=64)
+        p_scales = keep.tile([P, NPTS], U8, align_bytes=64)
+        nc.vector.quantize_mx(
+            out=p_codes[:].bitcast(FP8X4), scales=p_scales[:], in_=p_grouped[:].rearrange("p n t -> p (n t)")
+        )
+        xc = psum.tile([P, PACK, NPTS], F32, tag="aux", bufs=2)
+        for t in range(PACK):
+            nc.tensor.matmul_mx(
+                out=xc[:, t, :],
+                lhsT=wc1_codes[:, t * P : (t + 1) * P].bitcast(FP8X4),
+                lhsT_scale=wc1_scales[:, t * P : (t + 1) * P],
+                rhs=p_codes[:].bitcast(FP8X4),
+                rhs_scale=p_scales[:],
+                start=True,
+                stop=True,
+            )
+        result = keep.tile([P, PACK, NPTS], F32)
+        for t in range(PACK):
+            nc.scalar.activation(
+                out=result[:, t, :], in_=xc[:, t, :], func=ACT.Relu, bias=shift[1][:, t : t + 1], scale=gain[1][:, t : t + 1]
+            )
+        nc.sync.dma_start(out=out[0].rearrange("(m t) n -> m t n", t=PACK), in_=result[:])

@@ -23,11 +23,11 @@ LOADS = (UNIT,) * SHORT_LOADS + (2 * UNIT,) * ((UNITS - SHORT_LOADS) // 2)
 WC1_LOAD_AT = 12 * UNIT
 BANKS = UNITS * PACK
 AHEAD = 6
+READ_ORDER = (3, 0, 1, 2)
 GROUPED_BUFS = 2
-S_COLS = 336
+S_COLS = 352
 BN_EPS = 1e-5
-WC1_AT = 48
-EARLY = 3
+NORM2_AT = 16
 
 FLOPS = 2 * H * H * (COLS + NPTS)
 
@@ -54,10 +54,6 @@ def tile_p2b_xcorr_pb_kernel(tc, h2, W3, g3, b3, m3, v3, Wc1, gc1, bc1, mc1, vc1
 
         ident = keep.tile([P, P], F32)
         make_identity(nc, ident[:])
-        load_vector(nc.gpsimd, 7, vc1)
-        load_vector(nc.gpsimd, 1, gc1)
-        load_vector(nc.gpsimd, 3, bc1)
-        load_vector(nc.gpsimd, 5, mc1)
 
         w3_rows = keep.tile([P, PACK, H], BF16)
         nc.sync.dma_start(out=w3_rows[:], in_=W3.rearrange("(m t) h -> m t h", t=PACK))
@@ -74,6 +70,10 @@ def tile_p2b_xcorr_pb_kernel(tc, h2, W3, g3, b3, m3, v3, Wc1, gc1, bc1, mc1, vc1
             first += width
             if first == WC1_LOAD_AT:
                 nc.sync.dma_start(out=wc1_rows[:], in_=Wc1.rearrange("(m t) h -> m t h", t=PACK))
+                load_vector(nc.sync, 7, vc1)
+                load_vector(nc.sync, 1, gc1)
+                load_vector(nc.sync, 3, bc1)
+                load_vector(nc.sync, 5, mc1)
 
         one = keep.tile([P, 1], F32)
         nc.vector.memset(one[:], 1.0)
@@ -221,14 +221,14 @@ def tile_p2b_xcorr_pb_kernel(tc, h2, W3, g3, b3, m3, v3, Wc1, gc1, bc1, mc1, vc1
         def scalar_reads(s):
             return s % 3 == 2
 
-        def read_early(s):
-            if s < BANKS and scalar_reads(s):
-                t = s % PACK
-                h3 = keep.tile([P, UNIT], BF16, tag="h3", bufs=6)
-                nc.scalar.activation(
-                    out=h3[:], in_=bank_of[s][:], func=ACT.Relu, bias=shift[0][:, t : t + 1], scale=gain_abs[:, t : t + 1]
-                )
-                fresh.append((t, h3))
+        def read_at_once(s):
+            t = s % PACK
+            h3 = keep.tile([P, UNIT], BF16, tag="h3", bufs=6)
+            nc.scalar.activation(
+                out=h3[:], in_=bank_of[s][:], func=ACT.Relu, bias=shift[0][:, t : t + 1], scale=gain_abs[:, t : t + 1]
+            )
+            fresh.append((t, h3))
+            was_read.add(s)
 
         def fold():
             for t, h3 in ripe:
@@ -241,41 +241,45 @@ def tile_p2b_xcorr_pb_kernel(tc, h2, W3, g3, b3, m3, v3, Wc1, gc1, bc1, mc1, vc1
             if not scalar_reads(s):
                 running_max("x3", top, s % PACK, bank_of[s])
 
+        was_read = set()
+        issued = []
+
+        def refill():
+            while len(issued) < BANKS and len(issued) // PACK in codes_of and (len(issued) < AHEAD or len(issued) - AHEAD in was_read):
+                multiply(len(issued))
+                issued.append(len(issued))
+                if scalar_reads(issued[-1]):
+                    read_at_once(issued[-1])
+
+
         for u in range(GROUPED_BUFS):
             interleave_most(u)
         interleave_rest(0)
         quantize_weights(w3_grouped, w3_codes, w3_scales)
         quantize(0)
         interleave(GROUPED_BUFS)
-        for s in range(PACK):
-            multiply(s)
-        interleave_rest(1)
-        quantize(1)
-        interleave(GROUPED_BUFS + 1)
-        for s in range(PACK, AHEAD):
-            multiply(s)
+        refill()
 
-        for s in range(EARLY):
-            read_early(s)
-        for s in range(BANKS):
-            nxt = s + AHEAD
-            read_early(s + EARLY)
-            if nxt < BANKS and nxt % PACK == 0:
+        for r in range(UNITS):
+            nxt = r + 1
+            if nxt < UNITS:
+                if nxt < GROUPED_BUFS:
+                    interleave_rest(nxt)
                 fold()
-                quantize(nxt // PACK)
-                if nxt // PACK + GROUPED_BUFS < UNITS:
-                    interleave(nxt // PACK + GROUPED_BUFS)
-            read_bank(s)
-            if nxt < BANKS:
-                multiply(nxt)
-            if s == WC1_AT:
-                wc1_halves = turn_weights(wc1_rows)
+                quantize(nxt)
+                if nxt + GROUPED_BUFS < UNITS:
+                    interleave(nxt + GROUPED_BUFS)
+                refill()
+            for t in READ_ORDER:
+                read_bank(r * PACK + t)
+                was_read.add(r * PACK + t)
+                refill()
+            if r == NORM2_AT:
                 norm_root(1)
-            if s == WC1_AT + 2 * PACK:
-                wc1_grouped = group_weights(wc1_halves, nc.scalar.copy)
+            if r == NORM2_AT + 2:
                 norm_reciprocal(1)
-            if s == WC1_AT + 5 * PACK:
-                quantize_weights(wc1_grouped, wc1_codes, wc1_scales)
+            if r == UNITS - 2:
+                wc1_grouped = group_weights(turn_weights(wc1_rows), nc.scalar.copy)
         norm_gain_shift(1)
 
         fold()
@@ -299,6 +303,7 @@ def tile_p2b_xcorr_pb_kernel(tc, h2, W3, g3, b3, m3, v3, Wc1, gc1, bc1, mc1, vc1
             )
         peak_h3 = keep.tile([P, PACK, NPTS], BF16)
         nc.vector.tensor_tensor(out=peak_h3[:], in0=half_h3[:, :, 0:NPTS], in1=half_h3[:, :, NPTS : 2 * NPTS], op=ALU.max)
+        quantize_weights(wc1_grouped, wc1_codes, wc1_scales)
         pooled = keep.tile([P, PACK, NPTS], BF16)
         nc.vector.tensor_tensor(out=pooled[:], in0=pooled_x3[:], in1=peak_h3[:], op=ALU.max)
 

from contextlib import ExitStack

import concourse.mybir as mybir
from concourse.masks import make_identity

F32 = mybir.dt.float32
BF16 = mybir.dt.bfloat16
U32 = mybir.dt.uint32
U8 = mybir.dt.uint8
FP8X4 = mybir.dt.float8_e4m3fn_x4
ALU = mybir.AluOpType
ACT = mybir.ActivationFunctionType

P = 128
PACK = 4
H = 512
NPTS = 128
COLS = NPTS * NPTS
UNIT = 512
UNITS = COLS // UNIT
SHORT_LOADS = 6
LOADS = (UNIT,) * SHORT_LOADS + (2 * UNIT,) * ((UNITS - SHORT_LOADS) // 2)
WC1_LOAD_AT = 12 * UNIT
BANKS = UNITS * PACK
AHEAD = 6
READ_ORDER = (3, 0, 1, 2)
GROUPED_BUFS = 2
S_COLS = 352
BN_EPS = 1e-5
NORM2_AT = 16

FLOPS = 2 * H * H * (COLS + NPTS)


def tile_p2b_xcorr_pb_kernel(tc, h2, W3, g3, b3, m3, v3, Wc1, gc1, bc1, mc1, vc1, out):
    nc = tc.nc
    with ExitStack() as ctx:
        keep = ctx.enter_context(tc.tile_pool(name="keep", bufs=1))
        rawp = ctx.enter_context(tc.tile_pool(name="rawp", bufs=1))
        grpp = ctx.enter_context(tc.tile_pool(name="grpp", bufs=GROUPED_BUFS))
        codp = ctx.enter_context(tc.tile_pool(name="codp", bufs=3))
        psum = ctx.enter_context(tc.psum_pool(name="psum", bufs=AHEAD))
        ctx.enter_context(tc.manual_schedule())

        prm = keep.tile([P, 8, 16], BF16)

        def load_vector(queue, slot, vec):
            queue.dma_start(out=prm[:, slot, 0:PACK], in_=vec.rearrange("(p t) -> p t", t=PACK))

        load_vector(nc.scalar, 0, g3)
        load_vector(nc.scalar, 6, v3)
        load_vector(nc.scalar, 2, b3)
        load_vector(nc.scalar, 4, m3)

        ident = keep.tile([P, P], F32)
        make_identity(nc, ident[:])

        w3_rows = keep.tile([P, PACK, H], BF16)
        nc.sync.dma_start(out=w3_rows[:], in_=W3.rearrange("(m t) h -> m t h", t=PACK))
        wc1_rows = keep.tile([P, PACK, H], BF16)

        h2_rows = h2[0].rearrange("(p j) m n -> p j (m n)", j=PACK)
        raw_of = {}
        first = 0
        for width in LOADS:
            raw = rawp.tile([P, PACK, width], BF16, tag="raw%d" % width, bufs=SHORT_LOADS if width == UNIT else len(LOADS) - SHORT_LOADS)
            nc.sync.dma_start(out=raw[:], in_=h2_rows[:, :, first : first + width])
            for a in range(0, width, UNIT):
                raw_of[(first + a) // UNIT] = (raw, a)
            first += width
            if first == WC1_LOAD_AT:
                nc.sync.dma_start(out=wc1_rows[:], in_=Wc1.rearrange("(m t) h -> m t h", t=PACK))
                load_vector(nc.sync, 7, vc1)
                load_vector(nc.sync, 1, gc1)
                load_vector(nc.sync, 3, bc1)
                load_vector(nc.sync, 5, mc1)

        one = keep.tile([P, 1], F32)
        nc.vector.memset(one[:], 1.0)
        warm = keep.tile([P, 1], F32)
        nc.scalar.activation(out=warm[:], in_=one[:], func=ACT.Sqrt)

        sign = keep.tile([P, PACK], F32)
        nc.vector.tensor_scalar(out=sign[:], in0=prm[:, 0, 0:PACK], scalar1=0.0, scalar2=2.0, op0=ALU.is_ge, op1=ALU.mult)
        nc.vector.tensor_scalar(out=sign[:], in0=sign[:], scalar1=-1.0, scalar2=None, op0=ALU.add)

        var_eps, std, rough, newton, rstd, gain, shift = {}, {}, {}, {}, {}, {}, {}
        for k in range(2):
            var_eps[k] = keep.tile([P, PACK], F32, name="var_eps%d" % k)
            std[k] = keep.tile([P, PACK], F32, name="std%d" % k)
            rough[k] = keep.tile([P, PACK], F32, name="rough%d" % k)
            newton[k] = keep.tile([P, PACK], F32, name="newton%d" % k)
            rstd[k] = keep.tile([P, PACK], F32, name="rstd%d" % k)
            gain[k] = keep.tile([P, PACK], F32, name="gain%d" % k)
            shift[k] = keep.tile([P, PACK], F32, name="shift%d" % k)
        gain_abs = keep.tile([P, PACK], F32)

        def norm_root(k):
            nc.gpsimd.tensor_scalar(
                out=var_eps[k][:], in0=prm[:, 6 + k, 0:PACK], scalar1=1.0, scalar2=BN_EPS, op0=ALU.mult, op1=ALU.add
            )
            nc.scalar.activation(out=std[k][:], in_=var_eps[k][:], func=ACT.Sqrt)

        def norm_reciprocal(k):
            nc.vector.reciprocal(out=rough[k][:], in_=std[k][:])

        def norm_gain_shift(k):
            tt = nc.gpsimd.tensor_tensor
            tt(out=newton[k][:], in0=rough[k][:], in1=rough[k][:], op=ALU.mult)
            tt(out=newton[k][:], in0=newton[k][:], in1=var_eps[k][:], op=ALU.mult)
            nc.gpsimd.tensor_scalar(out=newton[k][:], in0=newton[k][:], scalar1=-0.5, scalar2=1.5, op0=ALU.mult, op1=ALU.add)
            tt(out=rstd[k][:], in0=rough[k][:], in1=newton[k][:], op=ALU.mult)
            tt(out=gain[k][:], in0=prm[:, k, 0:PACK], in1=rstd[k][:], op=ALU.mult)
            tt(out=shift[k][:], in0=prm[:, 4 + k, 0:PACK], in1=gain[k][:], op=ALU.mult)
            tt(out=shift[k][:], in0=prm[:, 2 + k, 0:PACK], in1=shift[k][:], op=ALU.subtract)

        norm_root(0)
        norm_reciprocal(0)
        norm_gain_shift(0)
        nc.gpsimd.tensor_tensor(out=gain_abs[:], in0=gain[0][:], in1=sign[:], op=ALU.mult)

        w3_signed = keep.tile([P, PACK, H], BF16)
        for t in range(PACK):
            nc.vector.tensor_scalar(
                out=w3_signed[:, t, :], in0=w3_rows[:, t, :], scalar1=sign[:, t : t + 1], scalar2=None, op0=ALU.mult
            )

        def turn_weights(rows):
            halves = []
            for b in range(2):
                turned = psum.tile([P, 2, 2, P], F32, tag="aux", bufs=2)
                for i in range(2):
                    words = rows[:, 2 * b + i, :].bitcast(F32)
                    for u in range(2):
                        nc.tensor.transpose(turned[:, i, u, :], words[:, u : H // 2 : 2], ident[:])
                halves.append(turned)
            return halves

        def group_weights(halves, copy):
            grouped_w = keep.tile([P, PACK * H], BF16, align_bytes=64)
            words_out = grouped_w[:].bitcast(F32).rearrange("p (t m u) -> p t m u", t=PACK, u=2)
            for b in range(2):
                copy(out=words_out[:, 2 * b : 2 * b + 2, :, :], in_=halves[b][:].rearrange("p t u m -> p t m u"))
            return grouped_w

        def quantize_weights(grouped_w, codes, scales):
            nc.vector.quantize_mx(out=codes[:].bitcast(FP8X4), scales=scales[:], in_=grouped_w[:])

        w3_codes = keep.tile([P, H], U32, align_bytes=64)
        w3_scales = keep.tile([P, H], U8, align_bytes=64)
        wc1_codes = keep.tile([P, H], U32, align_bytes=64)
        wc1_scales = keep.tile([P, H], U8, align_bytes=64)
        w3_grouped = group_weights(turn_weights(w3_signed), nc.vector.tensor_copy)

        grouped_of = {}
        codes_of = {}
        bank_of = {}

        def rows_of(u):
            raw, a = raw_of[u]
            return raw[:, :, a : a + UNIT].rearrange("p j c -> p c j")

        def interleave_most(u):
            grouped = grpp.tile([P, UNIT, PACK], BF16, tag="grouped", align_bytes=64)
            nc.scalar.copy(out=grouped[:, 0:S_COLS, :], in_=rows_of(u)[:, 0:S_COLS, :])
            grouped_of[u] = grouped

        def interleave_rest(u):
            if u < GROUPED_BUFS:
                nc.vector.tensor_copy(out=grouped_of[u][:, S_COLS:UNIT, :], in_=rows_of(u)[:, S_COLS:UNIT, :])
            else:
                nc.gpsimd.tensor_scalar(
                    out=grouped_of[u][:, S_COLS:UNIT, :],
                    in0=rows_of(u)[:, S_COLS:UNIT, :],
                    scalar1=1.0,
                    scalar2=0.0,
                    op0=ALU.mult,
                    op1=ALU.add,
                )

        def interleave(u):
            interleave_most(u)
            interleave_rest(u)

        def quantize(u):
            codes = codp.tile([P, UNIT], U32, tag="codes", align_bytes=64)
            scales = codp.tile([P, UNIT], U8, tag="scales", align_bytes=64)
            nc.vector.quantize_mx(
                out=codes[:].bitcast(FP8X4), scales=scales[:], in_=grouped_of[u][:].rearrange("p c j -> p (c j)")
            )
            codes_of[u] = (codes, scales)

        def multiply(s):
            u, t = divmod(s, PACK)
            codes, scales = codes_of[u]
            bank = psum.tile([P, UNIT], F32, tag="x3")
            nc.tensor.matmul_mx(
                out=bank[:],
                lhsT=w3_codes[:, t * P : (t + 1) * P].bitcast(FP8X4),
                lhsT_scale=w3_scales[:, t * P : (t + 1) * P],
                rhs=codes[:].bitcast(FP8X4),
                rhs_scale=scales[:],
                start=True,
                stop=True,
            )
            bank_of[s] = bank

        top = keep.tile([P, PACK, UNIT], F32)
        top_h3 = keep.tile([P, PACK, UNIT], BF16)
        started = set()
        fresh = []
        ripe = []

        def running_max(what, acc, t, new):
            if (what, t) in started:
                nc.vector.tensor_tensor(out=acc[:, t, :], in0=new[:], in1=acc[:, t, :], op=ALU.max)
            else:
                nc.vector.tensor_copy(out=acc[:, t, :], in_=new[:])
                started.add((what, t))

        def scalar_reads(s):
            return s % 3 == 2

        def read_at_once(s):
            t = s % PACK
            h3 = keep.tile([P, UNIT], BF16, tag="h3", bufs=6)
            nc.scalar.activation(
                out=h3[:], in_=bank_of[s][:], func=ACT.Relu, bias=shift[0][:, t : t + 1], scale=gain_abs[:, t : t + 1]
            )
            fresh.append((t, h3))
            was_read.add(s)

        def fold():
            for t, h3 in ripe:
                running_max("h3", top_h3, t, h3)
            ripe.clear()
            ripe.extend(fresh)
            fresh.clear()

        def read_bank(s):
            if not scalar_reads(s):
                running_max("x3", top, s % PACK, bank_of[s])

        was_read = set()
        issued = []

        def refill():
            while len(issued) < BANKS and len(issued) // PACK in codes_of and (len(issued) < AHEAD or len(issued) - AHEAD in was_read):
                multiply(len(issued))
                issued.append(len(issued))
                if scalar_reads(issued[-1]):
                    read_at_once(issued[-1])


        for u in range(GROUPED_BUFS):
            interleave_most(u)
        interleave_rest(0)
        quantize_weights(w3_grouped, w3_codes, w3_scales)
        quantize(0)
        interleave(GROUPED_BUFS)
        refill()

        for r in range(UNITS):
            nxt = r + 1
            if nxt < UNITS:
                if nxt < GROUPED_BUFS:
                    interleave_rest(nxt)
                fold()
                quantize(nxt)
                if nxt + GROUPED_BUFS < UNITS:
                    interleave(nxt + GROUPED_BUFS)
                refill()
            for t in READ_ORDER:
                read_bank(r * PACK + t)
                was_read.add(r * PACK + t)
                refill()
            if r == NORM2_AT:
                norm_root(1)
            if r == NORM2_AT + 2:
                norm_reciprocal(1)
            if r == UNITS - 2:
                wc1_grouped = group_weights(turn_weights(wc1_rows), nc.scalar.copy)
        norm_gain_shift(1)

        fold()
        fold()
        half_h3 = keep.tile([P, PACK, 2 * NPTS], BF16)
        nc.vector.tensor_tensor(out=half_h3[:], in0=top_h3[:, :, 0 : 2 * NPTS], in1=top_h3[:, :, 2 * NPTS : UNIT], op=ALU.max)
        half = keep.tile([P, PACK, 2 * NPTS], F32)
        peak = keep.tile([P, PACK, NPTS], F32)
        pooled_x3 = keep.tile([P, PACK, NPTS], BF16)
        for t in (0, 2):
            nc.vector.tensor_tensor(
                out=half[:, t : t + 2, :], in0=top[:, t : t + 2, 0 : 2 * NPTS], in1=top[:, t : t + 2, 2 * NPTS : UNIT], op=ALU.max
            )
        for t in (0, 2):
            nc.vector.tensor_tensor(
                out=peak[:, t : t + 2, :], in0=half[:, t : t + 2, 0:NPTS], in1=half[:, t : t + 2, NPTS : 2 * NPTS], op=ALU.max
            )
        for t in range(PACK):
            nc.scalar.activation(
                out=pooled_x3[:, t, :], in_=peak[:, t, :], func=ACT.Relu, bias=shift[0][:, t : t + 1], scale=gain_abs[:, t : t + 1]
            )
        peak_h3 = keep.tile([P, PACK, NPTS], BF16)
        nc.vector.tensor_tensor(out=peak_h3[:], in0=half_h3[:, :, 0:NPTS], in1=half_h3[:, :, NPTS : 2 * NPTS], op=ALU.max)
        quantize_weights(wc1_grouped, wc1_codes, wc1_scales)
        pooled = keep.tile([P, PACK, NPTS], BF16)
        nc.vector.tensor_tensor(out=pooled[:], in0=pooled_x3[:], in1=peak_h3[:], op=ALU.max)

        p_grouped = keep.tile([P, NPTS, PACK], BF16, align_bytes=64)
        nc.vector.tensor_copy(out=p_grouped[:], in_=pooled[:].rearrange("p t n -> p n t"))
        p_codes = keep.tile([P, NPTS], U32, align_bytes=64)
        p_scales = keep.tile([P, NPTS], U8, align_bytes=64)
        nc.vector.quantize_mx(
            out=p_codes[:].bitcast(FP8X4), scales=p_scales[:], in_=p_grouped[:].rearrange("p n t -> p (n t)")
        )
        xc = psum.tile([P, PACK, NPTS], F32, tag="aux", bufs=2)
        for t in range(PACK):
            nc.tensor.matmul_mx(
                out=xc[:, t, :],
                lhsT=wc1_codes[:, t * P : (t + 1) * P].bitcast(FP8X4),
                lhsT_scale=wc1_scales[:, t * P : (t + 1) * P],
                rhs=p_codes[:].bitcast(FP8X4),
                rhs_scale=p_scales[:],
                start=True,
                stop=True,
            )
        result = keep.tile([P, PACK, NPTS], F32)
        for t in range(PACK):
            nc.scalar.activation(
                out=result[:, t, :], in_=xc[:, t, :], func=ACT.Relu, bias=shift[1][:, t : t + 1], scale=gain[1][:, t : t + 1]
            )
        nc.sync.dma_start(out=out[0].rearrange("(m t) n -> m t n", t=PACK), in_=result[:])
